import numpy as np
import ml_dtypes


def mxq(x, axis, fmt="e4m3"):
    dtype, down = {"e4m3": (ml_dtypes.float8_e4m3fn, 7), "e5m2": (ml_dtypes.float8_e5m2, 14)}[fmt]
    v = np.moveaxis(np.asarray(x, np.float32).astype(ml_dtypes.bfloat16).astype(np.float64), axis, -1)
    blocks = v.reshape(v.shape[:-1] + (-1, 32))
    amax = np.abs(blocks).max(-1, keepdims=True)
    byte = np.maximum(np.where(amax > 0, np.frexp(amax)[1] - 1 + 127, 0) - down, 1)
    scale = np.exp2(byte - 127.0)
    codes = (blocks / scale).astype(np.float32).astype(dtype).astype(np.float64)
    return np.moveaxis((codes * scale).reshape(v.shape), -1, axis)


WIDE = False


def mx_kscale(k):
    if not WIDE:
        return np.ones(k)
    levels = np.array([10, -10, 5, -5, 0])
    a = np.random.permutation(np.resize(levels, k // 512 * 4)).reshape(k // 512, 4)
    idx = np.arange(k)
    return np.exp2(a[idx // 512, idx % 128 // 32])


BF16 = ml_dtypes.bfloat16


def bf(x):
    return np.asarray(x, np.float32).astype(BF16)


def f64(x):
    return np.asarray(x).astype(np.float64)


B, C, H, W = 2, 512, 16, 16
OFFSETS = [(-1, 0), (1, 0), (0, -1), (0, 1), (-1, -1), (-1, 1), (1, -1), (1, 1)]


def _neighbor_mean(x):
    p = np.pad(x, ((0, 0), (0, 0), (1, 1), (1, 1)), mode="edge")
    h, w = x.shape[2], x.shape[3]
    s = None
    for dy, dx in OFFSETS:
        sl = p[:, :, 1 + dy:1 + dy + h, 1 + dx:1 + dx + w]
        s = sl if s is None else s + sl
    return s / 8.0


def setup_inputs():
    s = mx_kscale(C)
    s = s / s.max()
    return {"x": bf(np.random.standard_normal((B, C, H, W)) * s[None, :, None, None]),
            "Wp": bf(np.random.standard_normal((C, 2 * C)) / np.sqrt(C) / np.concatenate([s, s])[None, :]),
            "b": bf(np.random.standard_normal(C) * 0.3)}


def reference(x, Wp, b):
    x, Wp, b = f64(x), f64(Wp), f64(b)
    n, c, h, w = x.shape
    mean = _neighbor_mean(x)
    xq = mxq(x, 1, "e4m3").reshape(n, c, h * w)
    mq = mxq(mean, 1, "e4m3").reshape(n, c, h * w)
    out = ((mxq(Wp[:, :c], 1, "e4m3") @ xq)
           + (mxq(Wp[:, c:], 1, "e4m3") @ mq)).reshape(n, c, h, w) + b[None, :, None, None]
    return np.maximum(out, 0.0) + x

@@ -1,0 +1,238 @@
+import concourse.mybir as mybir
+from concourse.masks import make_identity
+
+F32 = mybir.dt.float32
+BF16 = mybir.dt.bfloat16
+U32 = mybir.dt.uint32
+U8 = mybir.dt.uint8
+FP8X4 = mybir.dt.float8_e4m3fn_x4
+ADD = mybir.AluOpType.add
+MULT = mybir.AluOpType.mult
+MAX = mybir.AluOpType.max
+COPY = mybir.ActivationFunctionType.Copy
+IDENTITY = mybir.ActivationFunctionType.Identity
+
+P = 128
+PACK = 4
+BATCH = 2
+CHANNELS = P * PACK
+SIDE = 16
+PIXELS = SIDE * SIDE
+ROW = SIDE * PACK
+PADDED_ROW = (SIDE + 2) * PACK
+WORDS = CHANNELS // 2
+
+FLOPS = 2 * CHANNELS * (2 * CHANNELS) * (BATCH * PIXELS)
+
+
+def tile_staticgraphmodule_s_kernel(tc, x, Wp, b, out):
+    nc = tc.nc
+    with (
+        tc.tile_pool(name="keep", bufs=1) as keep,
+        tc.psum_pool(name="psum", bufs=1) as psum,
+        tc.manual_schedule(),
+    ):
+        x_raw = keep.tile([P, BATCH, PACK, PIXELS], BF16, name="x_raw")
+        x_pad = keep.tile([P, BATCH, SIDE + 2, ROW], BF16, name="x_pad", align_bytes=64)
+        up_down = keep.tile([P, BATCH, SIDE, ROW], F32, name="up_down")
+        up_down_8th = keep.tile([P, BATCH, SIDE, ROW], F32, name="up_down_8th")
+        column3 = keep.tile([P, BATCH, SIDE, PADDED_ROW], F32, name="column3")
+        sides = keep.tile([P, BATCH, SIDE, ROW], F32, name="sides")
+        mean = keep.tile([P, BATCH, SIDE, ROW], BF16, name="mean", align_bytes=64)
+        x_codes = keep.tile([P, BATCH, PIXELS], U32, name="x_codes", align_bytes=64)
+        x_scales = keep.tile([P, BATCH, PIXELS], U8, name="x_scales", align_bytes=64)
+        mean_codes = keep.tile([P, BATCH, PIXELS], U32, name="mean_codes", align_bytes=64)
+        mean_scales = keep.tile([P, BATCH, PIXELS], U8, name="mean_scales", align_bytes=64)
+        w_raw = keep.tile([P, PACK * 2 * CHANNELS], BF16, name="w_raw")
+        w_grouped = keep.tile([P, PACK * 2 * P * PACK], BF16, name="w_grouped", align_bytes=64)
+        w_codes = keep.tile([P, PACK * 2 * P], U32, name="w_codes", align_bytes=64)
+        w_scales = keep.tile([P, PACK * 2 * P], U8, name="w_scales", align_bytes=64)
+        identity = keep.tile([P, P], F32, name="identity")
+        b_raw = keep.tile([P, PACK], BF16, name="b_raw")
+        b_f32 = keep.tile([P, PACK], F32, name="b_f32")
+        minus_b = keep.tile([P, PACK], F32, name="minus_b")
+        x_plus_b = keep.tile([P, BATCH, PACK, PIXELS], F32, name="x_plus_b")
+        result = keep.tile([P, BATCH, PACK, PIXELS], F32, name="result")
+
+        w_words = w_raw[:].bitcast(F32)
+        w_grouped_words = w_grouped[:].bitcast(F32)
+        sums = {}
+
+        def regroup(n, copy):
+            copy(
+                out=x_pad[:, n, 1 : SIDE + 1, :].rearrange("p i (j t) -> p (i j) t", t=PACK),
+                in_=x_raw[:, n].rearrange("p t f -> p f t"),
+            )
+            copy(
+                out=x_pad[:, n, 0 : SIDE + 2 : SIDE + 1, :].rearrange(
+                    "p e (j t) -> p e j t", t=PACK
+                ),
+                in_=x_raw[:, n]
+                .rearrange("p t (i j) -> p t i j", j=SIDE)[:, :, 0 : SIDE : SIDE - 1, :]
+                .rearrange("p t e j -> p e j t"),
+            )
+
+        def quantise(codes, scales, values):
+            nc.vector.quantize_mx(out=codes.bitcast(FP8X4), scales=scales, in_=values)
+
+        def quantise_x(n):
+            quantise(
+                x_codes[:, n, :],
+                x_scales[:, n, :],
+                x_pad[:, n, 1 : SIDE + 1, :].rearrange("p i r -> p (i r)"),
+            )
+
+        def add_up_and_down(n):
+            nc.vector.tensor_tensor(
+                out=up_down[:, n],
+                in0=x_pad[:, n, 0:SIDE, :],
+                in1=x_pad[:, n, 2 : SIDE + 2, :],
+                op=ADD,
+            )
+            nc.scalar.activation(out=up_down_8th[:, n], in_=up_down[:, n], func=COPY, scale=0.125)
+
+        def add_centre(n):
+            nc.vector.tensor_tensor(
+                out=column3[:, n, :, PACK : PACK + ROW],
+                in0=up_down[:, n],
+                in1=x_pad[:, n, 1 : SIDE + 1, :],
+                op=ADD,
+            )
+            pixels = column3[:, n].rearrange("p i (j t) -> p i j t", t=PACK)
+            nc.scalar.copy(
+                out=pixels[:, :, 0 : SIDE + 2 : SIDE + 1, :],
+                in_=pixels[:, :, 1 : SIDE + 1 : SIDE - 1, :],
+            )
+
+        def add_left_and_right(n):
+            nc.vector.tensor_tensor(
+                out=sides[:, n],
+                in0=column3[:, n, :, 0:ROW],
+                in1=column3[:, n, :, 2 * PACK : 2 * PACK + ROW],
+                op=ADD,
+            )
+
+        def finish_mean(n):
+            nc.vector.scalar_tensor_tensor(
+                out=mean[:, n].rearrange("p i r -> p (i r)"),
+                in0=sides[:, n].rearrange("p i r -> p (i r)"),
+                scalar=0.125,
+                in1=up_down_8th[:, n].rearrange("p i r -> p (i r)"),
+                op0=MULT,
+                op1=ADD,
+            )
+
+        def quantise_mean(n):
+            quantise(
+                mean_codes[:, n, :],
+                mean_scales[:, n, :],
+                mean[:, n].rearrange("p i r -> p (i r)"),
+            )
+
+        def transpose_weights(t):
+            turned = psum.tile([P, 2, 2, P], F32, name="turned%d" % t, tag="bank%d" % t)
+            for s in range(2):
+                for u in range(2):
+                    first = (2 * t + s) * WORDS + u
+                    nc.tensor.transpose(
+                        out=turned[:, s, u, :],
+                        in_=w_words[:, first : (2 * t + s + 1) * WORDS : 2],
+                        identity=identity[:],
+                    )
+            nc.scalar.copy(
+                out=w_grouped_words[:, 2 * t * WORDS : 2 * (t + 1) * WORDS].rearrange(
+                    "q (s o u) -> q s o u", s=2, u=2
+                ),
+                in_=turned[:].rearrange("q s u o -> q s o u"),
+            )
+
+        def quantise_weights(half):
+            words = slice(half * 4 * P, (half + 1) * 4 * P)
+            values = slice(half * 4 * P * PACK, (half + 1) * 4 * P * PACK)
+            quantise(w_codes[:, words], w_scales[:, words], w_grouped[:, values])
+
+        def multiply(n, t, s, codes, scales):
+            columns = slice((2 * t + s) * P, (2 * t + s + 1) * P)
+            nc.tensor.matmul_mx(
+                out=sums[(n, t)][:],
+                lhsT=w_codes[:, columns].bitcast(FP8X4),
+                lhsT_scale=w_scales[:, columns],
+                rhs=codes[:, n, :].bitcast(FP8X4),
+                rhs_scale=scales[:, n, :],
+                start=(s == 0),
+                stop=(s == 1),
+            )
+
+        def finish(n, t):
+            nc.vector.scalar_tensor_tensor(
+                out=result[:, n, t, :],
+                in0=sums[(n, t)][:],
+                scalar=minus_b[:, t : t + 1],
+                in1=x_plus_b[:, n, t, :],
+                op0=MAX,
+                op1=ADD,
+            )
+            nc.sync.dma_start(
+                out=out[n].rearrange("(p t) h w -> p t (h w)", t=PACK)[:, t, :],
+                in_=result[:, n, t, :],
+            )
+
+        nc.scalar.dma_start(out=b_raw[:], in_=b.rearrange("(p t) -> p t", t=PACK))
+        for n in range(BATCH):
+            nc.sync.dma_start(
+                out=x_raw[:, n], in_=x[n].rearrange("(p t) h w -> p t (h w)", t=PACK)
+            )
+        w_rows = Wp.rearrange("(p t) k -> p t k", t=PACK)
+        for half in range(2):
+            nc.sync.dma_start(
+                out=w_raw[:, half * 4 * CHANNELS : (half + 1) * 4 * CHANNELS].rearrange(
+                    "p (t k) -> p t k", t=2
+                ),
+                in_=w_rows[:, 2 * half : 2 * half + 2, :],
+            )
+        make_identity(nc, identity[:])
+        nc.scalar.activation(out=b_f32[:], in_=b_raw[:], func=COPY)
+        nc.scalar.activation(out=minus_b[:], in_=b_raw[:], func=COPY, scale=-1.0)
+
+        regroup(0, nc.vector.tensor_copy)
+        regroup(1, nc.scalar.copy)
+        add_up_and_down(0)
+        quantise_x(0)
+        add_centre(0)
+        transpose_weights(0)
+        transpose_weights(1)
+        add_up_and_down(1)
+        quantise_x(1)
+        add_left_and_right(0)
+        transpose_weights(2)
+        transpose_weights(3)
+        add_centre(1)
+        quantise_weights(0)
+        finish_mean(0)
+        quantise_weights(1)
+        for t in range(PACK):
+            for n in range(BATCH):
+                sums[(n, t)] = psum.tile(
+                    [P, PIXELS], F32, name="sums%d%d" % (n, t), tag="bank%d" % (PACK * n + t)
+                )
+                multiply(n, t, 0, x_codes, x_scales)
+        add_left_and_right(1)
+        quantise_mean(0)
+        for t in range(PACK):
+            multiply(0, t, 1, mean_codes, mean_scales)
+        for t in range(PACK):
+            nc.scalar.activation(
+                out=x_plus_b[:, :, t, :],
+                in_=x_raw[:, :, t, :],
+                func=IDENTITY,
+                bias=b_f32[:, t : t + 1],
+            )
+        finish_mean(1)
+        finish(0, 0)
+        quantise_mean(1)
+        for t in range(PACK):
+            multiply(1, t, 1, mean_codes, mean_scales)
+        for t in range(1, PACK):
+            finish(0, t)
+        for t in range(PACK):
+            finish(1, t)

@@ -11,6 +11,7 @@ MULT = mybir.AluOpType.mult
 MAX = mybir.AluOpType.max
 COPY = mybir.ActivationFunctionType.Copy
 IDENTITY = mybir.ActivationFunctionType.Identity
+RELU = mybir.ActivationFunctionType.Relu
 
 P = 128
 PACK = 4
@@ -19,8 +20,11 @@ CHANNELS = P * PACK
 SIDE = 16
 PIXELS = SIDE * SIDE
 ROW = SIDE * PACK
-PADDED_ROW = (SIDE + 2) * PACK
 WORDS = CHANNELS // 2
+BLOCK_ROWS = P // SIDE
+INNER_ROWS = BLOCK_ROWS - 2
+BAND_ROWS = (SIDE - 2 * INNER_ROWS) // 2
+LAST = PACK - 1
 
 FLOPS = 2 * CHANNELS * (2 * CHANNELS) * (BATCH * PIXELS)
 
@@ -34,10 +38,8 @@ def tile_staticgraphmodule_s_kernel(tc, x, Wp, b, out):
     ):
         x_raw = keep.tile([P, BATCH, PACK, PIXELS], BF16, name="x_raw")
         x_pad = keep.tile([P, BATCH, SIDE + 2, ROW], BF16, name="x_pad", align_bytes=64)
-        up_down = keep.tile([P, BATCH, SIDE, ROW], F32, name="up_down")
-        up_down_8th = keep.tile([P, BATCH, SIDE, ROW], F32, name="up_down_8th")
-        column3 = keep.tile([P, BATCH, SIDE, PADDED_ROW], F32, name="column3")
-        sides = keep.tile([P, BATCH, SIDE, ROW], F32, name="sides")
+        x_by_pixel = keep.tile([P, BATCH, 2, PACK, P], BF16, name="x_by_pixel")
+        matrix = keep.tile([P, INNER_ROWS * SIDE], BF16, name="matrix")
         mean = keep.tile([P, BATCH, SIDE, ROW], BF16, name="mean", align_bytes=64)
         x_codes = keep.tile([P, BATCH, PIXELS], U32, name="x_codes", align_bytes=64)
         x_scales = keep.tile([P, BATCH, PIXELS], U8, name="x_scales", align_bytes=64)
@@ -47,23 +49,82 @@ def tile_staticgraphmodule_s_kernel(tc, x, Wp, b, out):
         w_grouped = keep.tile([P, PACK * 2 * P * PACK], BF16, name="w_grouped", align_bytes=64)
         w_codes = keep.tile([P, PACK * 2 * P], U32, name="w_codes", align_bytes=64)
         w_scales = keep.tile([P, PACK * 2 * P], U8, name="w_scales", align_bytes=64)
-        identity = keep.tile([P, P], F32, name="identity")
+        identity_bf16 = keep.tile([P, P], BF16, name="identity_bf16")
+        identity_f32 = keep.tile([P, P], F32, name="identity_f32")
         b_raw = keep.tile([P, PACK], BF16, name="b_raw")
         b_f32 = keep.tile([P, PACK], F32, name="b_f32")
         minus_b = keep.tile([P, PACK], F32, name="minus_b")
-        x_plus_b = keep.tile([P, BATCH, PACK, PIXELS], F32, name="x_plus_b")
-        result = keep.tile([P, BATCH, PACK, PIXELS], F32, name="result")
+        x_plus_b = keep.tile([P, LAST, BATCH, PIXELS], F32, name="x_plus_b")
+        relu = keep.tile([P, BATCH, PIXELS], F32, name="relu")
+        result = keep.tile([P, PACK, BATCH, PIXELS], F32, name="result")
 
         w_words = w_raw[:].bitcast(F32)
         w_grouped_words = w_grouped[:].bitcast(F32)
         sums = {}
 
-        def regroup(n, copy):
-            copy(
+        def mean_by_adds(name, images, first_row, rows, pack, target):
+            groups = images.shape[1]
+            width = SIDE * pack
+            shape = [P, groups, rows, width]
+            return {
+                "above": images[:, :, first_row : first_row + rows, :],
+                "centre": images[:, :, first_row + 1 : first_row + 1 + rows, :],
+                "below": images[:, :, first_row + 2 : first_row + 2 + rows, :],
+                "target": target,
+                "pack": pack,
+                "width": width,
+                "up_down": keep.tile(shape, F32, name=name + "_up_down"),
+                "up_down_8th": keep.tile(shape, F32, name=name + "_up_down_8th"),
+                "column3": keep.tile([P, groups, rows, width + 2 * pack], F32, name=name + "_column3"),
+                "sides": keep.tile(shape, F32, name=name + "_sides"),
+            }
+
+        def add_up_and_down(work):
+            nc.vector.tensor_tensor(
+                out=work["up_down"][:], in0=work["above"], in1=work["below"], op=ADD
+            )
+            nc.scalar.activation(
+                out=work["up_down_8th"][:], in_=work["up_down"][:], func=COPY, scale=0.125
+            )
+
+        def add_centre(work):
+            pack = work["pack"]
+            nc.vector.tensor_tensor(
+                out=work["column3"][:, :, :, pack : pack + work["width"]],
+                in0=work["up_down"][:],
+                in1=work["centre"],
+                op=ADD,
+            )
+            pixels = work["column3"][:].rearrange("p g i (j t) -> p (g i) j t", t=pack)
+            nc.scalar.copy(
+                out=pixels[:, :, 0 : SIDE + 2 : SIDE + 1, :],
+                in_=pixels[:, :, 1 : SIDE + 1 : SIDE - 1, :],
+            )
+
+        def add_left_and_right(work):
+            nc.vector.tensor_tensor(
+                out=work["sides"][:],
+                in0=work["column3"][:, :, :, 0 : work["width"]],
+                in1=work["column3"][:, :, :, 2 * work["pack"] : 2 * work["pack"] + work["width"]],
+                op=ADD,
+            )
+
+        def finish_mean(work):
+            nc.vector.scalar_tensor_tensor(
+                out=work["target"],
+                in0=work["sides"][:].rearrange("p g i r -> p g (i r)"),
+                scalar=0.125,
+                in1=work["up_down_8th"][:].rearrange("p g i r -> p g (i r)"),
+                op0=MULT,
+                op1=ADD,
+            )
+
+        def regroup(n):
+            nc.vector.tensor_copy(
                 out=x_pad[:, n, 1 : SIDE + 1, :].rearrange("p i (j t) -> p (i j) t", t=PACK),
                 in_=x_raw[:, n].rearrange("p t f -> p f t"),
             )
-            copy(
+            nc.vector.tensor_copy(
                 out=x_pad[:, n, 0 : SIDE + 2 : SIDE + 1, :].rearrange(
                     "p e (j t) -> p e j t", t=PACK
                 ),
@@ -82,46 +143,6 @@ def tile_staticgraphmodule_s_kernel(tc, x, Wp, b, out):
                 x_pad[:, n, 1 : SIDE + 1, :].rearrange("p i r -> p (i r)"),
             )
 
-        def add_up_and_down(n):
-            nc.vector.tensor_tensor(
-                out=up_down[:, n],
-                in0=x_pad[:, n, 0:SIDE, :],
-                in1=x_pad[:, n, 2 : SIDE + 2, :],
-                op=ADD,
-            )
-            nc.scalar.activation(out=up_down_8th[:, n], in_=up_down[:, n], func=COPY, scale=0.125)
-
-        def add_centre(n):
-            nc.vector.tensor_tensor(
-                out=column3[:, n, :, PACK : PACK + ROW],
-                in0=up_down[:, n],
-                in1=x_pad[:, n, 1 : SIDE + 1, :],
-                op=ADD,
-            )
-            pixels = column3[:, n].rearrange("p i (j t) -> p i j t", t=PACK)
-            nc.scalar.copy(
-                out=pixels[:, :, 0 : SIDE + 2 : SIDE + 1, :],
-                in_=pixels[:, :, 1 : SIDE + 1 : SIDE - 1, :],
-            )
-
-        def add_left_and_right(n):
-            nc.vector.tensor_tensor(
-                out=sides[:, n],
-                in0=column3[:, n, :, 0:ROW],
-                in1=column3[:, n, :, 2 * PACK : 2 * PACK + ROW],
-                op=ADD,
-            )
-
-        def finish_mean(n):
-            nc.vector.scalar_tensor_tensor(
-                out=mean[:, n].rearrange("p i r -> p (i r)"),
-                in0=sides[:, n].rearrange("p i r -> p (i r)"),
-                scalar=0.125,
-                in1=up_down_8th[:, n].rearrange("p i r -> p (i r)"),
-                op0=MULT,
-                op1=ADD,
-            )
-
         def quantise_mean(n):
             quantise(
                 mean_codes[:, n, :],
@@ -129,15 +150,57 @@ def tile_staticgraphmodule_s_kernel(tc, x, Wp, b, out):
                 mean[:, n].rearrange("p i r -> p (i r)"),
             )
 
-        def transpose_weights(t):
-            turned = psum.tile([P, 2, 2, P], F32, name="turned%d" % t, tag="bank%d" % t)
+        def turn_x(n):
+            for block in range(2):
+                turned = psum.tile(
+                    [P, PACK, P],
+                    BF16,
+                    name="x_turned%d%d" % (n, block),
+                    tag="bank%d" % (2 * n + block),
+                )
+                first = (BAND_ROWS - 1 + block * INNER_ROWS) * SIDE
+                for t in range(PACK):
+                    nc.tensor.transpose(
+                        out=turned[:, t, :],
+                        in_=x_raw[:, n, t, first : first + P],
+                        identity=identity_bf16[:],
+                    )
+                nc.scalar.copy(out=x_by_pixel[:, n, block], in_=turned[:])
+
+        def mean_by_matrix(n):
+            for block in range(2):
+                means = psum.tile(
+                    [P, PACK, INNER_ROWS * SIDE],
+                    F32,
+                    name="means%d%d" % (n, block),
+                    tag="bank%d" % (2 * n + block),
+                )
+                for t in range(PACK):
+                    nc.tensor.matmul(
+                        out=means[:, t, :],
+                        lhsT=x_by_pixel[:, n, block, t, :],
+                        rhs=matrix[:],
+                        start=True,
+                        stop=True,
+                    )
+                first_row = BAND_ROWS + block * INNER_ROWS
+                copy = nc.scalar.copy if block == 0 else nc.vector.tensor_copy
+                copy(
+                    out=mean[:, n, first_row : first_row + INNER_ROWS, :].rearrange(
+                        "p i (j t) -> p (i j) t", t=PACK
+                    ),
+                    in_=means[:].rearrange("p t m -> p m t"),
+                )
+
+        def turn_weights(t):
+            turned = psum.tile([P, 2, 2, P], F32, name="w_turned%d" % t, tag="bank%d" % (PACK + t))
             for s in range(2):
                 for u in range(2):
                     first = (2 * t + s) * WORDS + u
                     nc.tensor.transpose(
                         out=turned[:, s, u, :],
                         in_=w_words[:, first : (2 * t + s + 1) * WORDS : 2],
-                        identity=identity[:],
+                        identity=identity_f32[:],
                     )
             nc.scalar.copy(
                 out=w_grouped_words[:, 2 * t * WORDS : 2 * (t + 1) * WORDS].rearrange(
@@ -151,30 +214,46 @@ def tile_staticgraphmodule_s_kernel(tc, x, Wp, b, out):
             values = slice(half * 4 * P * PACK, (half + 1) * 4 * P * PACK)
             quantise(w_codes[:, words], w_scales[:, words], w_grouped[:, values])
 
-        def multiply(n, t, s, codes, scales):
+        def multiply(t, s, codes, scales):
             columns = slice((2 * t + s) * P, (2 * t + s + 1) * P)
             nc.tensor.matmul_mx(
-                out=sums[(n, t)][:],
+                out=sums[t][:],
                 lhsT=w_codes[:, columns].bitcast(FP8X4),
                 lhsT_scale=w_scales[:, columns],
-                rhs=codes[:, n, :].bitcast(FP8X4),
-                rhs_scale=scales[:, n, :],
+                rhs=codes[:].rearrange("p n f -> p (n f)").bitcast(FP8X4),
+                rhs_scale=scales[:].rearrange("p n f -> p (n f)"),
                 start=(s == 0),
                 stop=(s == 1),
             )
 
-        def finish(n, t):
+        def add_bias_to_x(t):
+            nc.scalar.activation(
+                out=x_plus_b[:, t], in_=x_raw[:, :, t, :], func=IDENTITY, bias=b_f32[:, t : t + 1]
+            )
+
+        def finish(t):
             nc.vector.scalar_tensor_tensor(
-                out=result[:, n, t, :],
-                in0=sums[(n, t)][:],
+                out=result[:, t].rearrange("p n f -> p (n f)"),
+                in0=sums[t][:],
                 scalar=minus_b[:, t : t + 1],
-                in1=x_plus_b[:, n, t, :],
+                in1=x_plus_b[:, t].rearrange("p n f -> p (n f)"),
                 op0=MAX,
                 op1=ADD,
             )
             nc.sync.dma_start(
-                out=out[n].rearrange("(p t) h w -> p t (h w)", t=PACK)[:, t, :],
-                in_=result[:, n, t, :],
+                out=out.rearrange("n (p t) h w -> p t n (h w)", t=PACK)[:, t], in_=result[:, t]
+            )
+
+        def finish_beside(t):
+            nc.scalar.activation(
+                out=relu[:].rearrange("p n f -> p (n f)"),
+                in_=sums[t][:],
+                func=RELU,
+                bias=b_f32[:, t : t + 1],
+            )
+            nc.gpsimd.tensor_tensor(out=result[:, t], in0=relu[:], in1=x_raw[:, :, t, :], op=ADD)
+            nc.scalar.dma_start(
+                out=out.rearrange("n (p t) h w -> p t n (h w)", t=PACK)[:, t], in_=result[:, t]
             )
 
         nc.scalar.dma_start(out=b_raw[:], in_=b.rearrange("(p t) -> p t", t=PACK))
@@ -190,49 +269,70 @@ def tile_staticgraphmodule_s_kernel(tc, x, Wp, b, out):
                 ),
                 in_=w_rows[:, 2 * half : 2 * half + 2, :],
             )
-        make_identity(nc, identity[:])
+
+        make_identity(nc, identity_bf16[:])
+        make_identity(nc, identity_f32[:])
+        unit_images = mean_by_adds(
+            "matrix",
+            identity_bf16[:].rearrange("k (g i j) -> k g i j", g=1, j=SIDE),
+            0,
+            INNER_ROWS,
+            1,
+            matrix[:].rearrange("k (g m) -> k g m", g=1),
+        )
+        add_up_and_down(unit_images)
+        add_centre(unit_images)
+        add_left_and_right(unit_images)
+        finish_mean(unit_images)
         nc.scalar.activation(out=b_f32[:], in_=b_raw[:], func=COPY)
         nc.scalar.activation(out=minus_b[:], in_=b_raw[:], func=COPY, scale=-1.0)
 
-        regroup(0, nc.vector.tensor_copy)
-        regroup(1, nc.scalar.copy)
-        add_up_and_down(0)
-        quantise_x(0)
-        add_centre(0)
-        transpose_weights(0)
-        transpose_weights(1)
-        add_up_and_down(1)
-        quantise_x(1)
-        add_left_and_right(0)
-        transpose_weights(2)
-        transpose_weights(3)
-        add_centre(1)
-        quantise_weights(0)
-        finish_mean(0)
-        quantise_weights(1)
-        for t in range(PACK):
-            for n in range(BATCH):
-                sums[(n, t)] = psum.tile(
-                    [P, PIXELS], F32, name="sums%d%d" % (n, t), tag="bank%d" % (PACK * n + t)
-                )
-                multiply(n, t, 0, x_codes, x_scales)
-        add_left_and_right(1)
-        quantise_mean(0)
-        for t in range(PACK):
-            multiply(0, t, 1, mean_codes, mean_scales)
-        for t in range(PACK):
-            nc.scalar.activation(
-                out=x_plus_b[:, :, t, :],
-                in_=x_raw[:, :, t, :],
-                func=IDENTITY,
-                bias=b_f32[:, t : t + 1],
+        turn_x(0)
+        regroup(0)
+        turn_x(1)
+        regroup(1)
+        add_bias_to_x(0)
+        bands = [
+            mean_by_adds(
+                name,
+                x_pad[:],
+                first_row,
+                BAND_ROWS,
+                PACK,
+                mean[:, :, first_row : first_row + BAND_ROWS, :].rearrange("p n i r -> p n (i r)"),
             )
-        finish_mean(1)
-        finish(0, 0)
+            for name, first_row in (("top", 0), ("bottom", SIDE - BAND_ROWS))
+        ]
+        for band in bands:
+            add_up_and_down(band)
+        quantise_x(0)
+        turn_weights(0)
+        for band in bands:
+            add_centre(band)
+        quantise_x(1)
+        turn_weights(1)
+        for band in bands:
+            add_left_and_right(band)
+        turn_weights(2)
+        turn_weights(3)
+        quantise_weights(0)
+        for band in bands:
+            finish_mean(band)
+        quantise_weights(1)
+        mean_by_matrix(0)
+        mean_by_matrix(1)
+        for t in range(PACK):
+            sums[t] = psum.tile(
+                [P, BATCH * PIXELS], F32, name="sums%d" % t, tag="bank%d" % (PACK + t)
+            )
+            multiply(t, 0, x_codes, x_scales)
+        quantise_mean(0)
         quantise_mean(1)
-        for t in range(PACK):
-            multiply(1, t, 1, mean_codes, mean_scales)
-        for t in range(1, PACK):
-            finish(0, t)
-        for t in range(PACK):
-            finish(1, t)
+        multiply(LAST, 1, mean_codes, mean_scales)
+        for t in range(LAST):
+            multiply(t, 1, mean_codes, mean_scales)
+        add_bias_to_x(1)
+        add_bias_to_x(2)
+        finish_beside(LAST)
+        for t in range(LAST):
+            finish(t)

@@ -56,8 +56,9 @@ def tile_staticgraphmodule_s_kernel(tc, x, Wp, b, out):
         minus_b = keep.tile([P, PACK], F32, name="minus_b")
         x_plus_b = keep.tile([P, LAST, BATCH, PIXELS], F32, name="x_plus_b")
         relu = keep.tile([P, BATCH, PIXELS], F32, name="relu")
-        result = keep.tile([P, PACK, BATCH, PIXELS], F32, name="result")
+        result = keep.tile([P, BATCH, PACK, PIXELS], F32, name="result")
 
+        out_rows = [out[n].rearrange("(p t) h w -> p t (h w)", t=PACK) for n in range(BATCH)]
         w_words = w_raw[:].bitcast(F32)
         w_grouped_words = w_grouped[:].bitcast(F32)
         sums = {}
@@ -83,9 +84,6 @@ def tile_staticgraphmodule_s_kernel(tc, x, Wp, b, out):
             nc.vector.tensor_tensor(
                 out=work["up_down"][:], in0=work["above"], in1=work["below"], op=ADD
             )
-            nc.scalar.activation(
-                out=work["up_down_8th"][:], in_=work["up_down"][:], func=COPY, scale=0.125
-            )
 
         def add_centre(work):
             pack = work["pack"]
@@ -95,8 +93,15 @@ def tile_staticgraphmodule_s_kernel(tc, x, Wp, b, out):
                 in1=work["centre"],
                 op=ADD,
             )
-            pixels = work["column3"][:].rearrange("p g i (j t) -> p (g i) j t", t=pack)
-            nc.scalar.copy(
+
+        def divide_up_down(work):
+            nc.vector.tensor_scalar_mul(
+                out=work["up_down_8th"][:], in0=work["up_down"][:], scalar1=0.125
+            )
+
+        def repeat_end_columns(work):
+            pixels = work["column3"][:].rearrange("p g i (j t) -> p (g i) j t", t=work["pack"])
+            nc.vector.tensor_copy(
                 out=pixels[:, :, 0 : SIDE + 2 : SIDE + 1, :],
                 in_=pixels[:, :, 1 : SIDE + 1 : SIDE - 1, :],
             )
@@ -121,8 +126,8 @@ def tile_staticgraphmodule_s_kernel(tc, x, Wp, b, out):
 
         def regroup(n):
             nc.vector.tensor_copy(
-                out=x_pad[:, n, 1 : SIDE + 1, :].rearrange("p i (j t) -> p (i j) t", t=PACK),
-                in_=x_raw[:, n].rearrange("p t f -> p f t"),
+                out=x_pad[:, n, 1 : SIDE + 1, :].rearrange("p r (c i t) -> p (r c) t i", i=4, t=PACK),
+                in_=x_raw[:, n].rearrange("p t (c i) -> p c t i", i=4),
             )
             nc.vector.tensor_copy(
                 out=x_pad[:, n, 0 : SIDE + 2 : SIDE + 1, :].rearrange(
@@ -184,8 +189,7 @@ def tile_staticgraphmodule_s_kernel(tc, x, Wp, b, out):
                         stop=True,
                     )
                 first_row = BAND_ROWS + block * INNER_ROWS
-                copy = nc.scalar.copy if block == 0 else nc.vector.tensor_copy
-                copy(
+                nc.scalar.copy(
                     out=mean[:, n, first_row : first_row + INNER_ROWS, :].rearrange(
                         "p i (j t) -> p (i j) t", t=PACK
                     ),
@@ -214,14 +218,19 @@ def tile_staticgraphmodule_s_kernel(tc, x, Wp, b, out):
             values = slice(half * 4 * P * PACK, (half + 1) * 4 * P * PACK)
             quantise(w_codes[:, words], w_scales[:, words], w_grouped[:, values])
 
-        def multiply(t, s, codes, scales):
+        def multiply(n, t, s):
+            if s == 0:
+                sums[(n, t)] = psum.tile(
+                    [P, PIXELS], F32, name="sums%d%d" % (n, t), tag="bank%d" % (PACK * (1 - n) + t)
+                )
+            codes, scales = ((x_codes, x_scales), (mean_codes, mean_scales))[s]
             columns = slice((2 * t + s) * P, (2 * t + s + 1) * P)
             nc.tensor.matmul_mx(
-                out=sums[t][:],
+                out=sums[(n, t)][:],
                 lhsT=w_codes[:, columns].bitcast(FP8X4),
                 lhsT_scale=w_scales[:, columns],
-                rhs=codes[:].rearrange("p n f -> p (n f)").bitcast(FP8X4),
-                rhs_scale=scales[:].rearrange("p n f -> p (n f)"),
+                rhs=codes[:, n, :].bitcast(FP8X4),
+                rhs_scale=scales[:, n, :],
                 start=(s == 0),
                 stop=(s == 1),
             )
@@ -231,30 +240,28 @@ def tile_staticgraphmodule_s_kernel(tc, x, Wp, b, out):
                 out=x_plus_b[:, t], in_=x_raw[:, :, t, :], func=IDENTITY, bias=b_f32[:, t : t + 1]
             )
 
-        def finish(t):
+        def finish(n, t):
             nc.vector.scalar_tensor_tensor(
-                out=result[:, t].rearrange("p n f -> p (n f)"),
-                in0=sums[t][:],
+                out=result[:, n, t, :],
+                in0=sums[(n, t)][:],
                 scalar=minus_b[:, t : t + 1],
-                in1=x_plus_b[:, t].rearrange("p n f -> p (n f)"),
+                in1=x_plus_b[:, t, n, :],
                 op0=MAX,
                 op1=ADD,
             )
-            nc.sync.dma_start(
-                out=out.rearrange("n (p t) h w -> p t n (h w)", t=PACK)[:, t], in_=result[:, t]
-            )
+            nc.sync.dma_start(out=out_rows[n][:, t, :], in_=result[:, n, t, :])
 
-        def finish_beside(t):
+        def finish_beside(n):
             nc.scalar.activation(
-                out=relu[:].rearrange("p n f -> p (n f)"),
-                in_=sums[t][:],
+                out=relu[:, n, :],
+                in_=sums[(n, LAST)][:],
                 func=RELU,
-                bias=b_f32[:, t : t + 1],
+                bias=b_f32[:, LAST : LAST + 1],
             )
-            nc.gpsimd.tensor_tensor(out=result[:, t], in0=relu[:], in1=x_raw[:, :, t, :], op=ADD)
-            nc.scalar.dma_start(
-                out=out.rearrange("n (p t) h w -> p t n (h w)", t=PACK)[:, t], in_=result[:, t]
+            nc.gpsimd.tensor_tensor(
+                out=result[:, n, LAST, :], in0=relu[:, n, :], in1=x_raw[:, n, LAST, :], op=ADD
             )
+            nc.scalar.dma_start(out=out_rows[n][:, LAST, :], in_=result[:, n, LAST, :])
 
         nc.scalar.dma_start(out=b_raw[:], in_=b.rearrange("(p t) -> p t", t=PACK))
         for n in range(BATCH):
@@ -282,6 +289,8 @@ def tile_staticgraphmodule_s_kernel(tc, x, Wp, b, out):
         )
         add_up_and_down(unit_images)
         add_centre(unit_images)
+        divide_up_down(unit_images)
+        repeat_end_columns(unit_images)
         add_left_and_right(unit_images)
         finish_mean(unit_images)
         nc.scalar.activation(out=b_f32[:], in_=b_raw[:], func=COPY)
@@ -306,11 +315,16 @@ def tile_staticgraphmodule_s_kernel(tc, x, Wp, b, out):
         for band in bands:
             add_up_and_down(band)
         quantise_x(0)
-        turn_weights(0)
         for band in bands:
             add_centre(band)
-        quantise_x(1)
+        turn_weights(0)
         turn_weights(1)
+        add_bias_to_x(1)
+        for band in bands:
+            divide_up_down(band)
+        for band in bands:
+            repeat_end_columns(band)
+        quantise_x(1)
         for band in bands:
             add_left_and_right(band)
         turn_weights(2)
@@ -321,18 +335,17 @@ def tile_staticgraphmodule_s_kernel(tc, x, Wp, b, out):
         quantise_weights(1)
         mean_by_matrix(0)
         mean_by_matrix(1)
-        for t in range(PACK):
-            sums[t] = psum.tile(
-                [P, BATCH * PIXELS], F32, name="sums%d" % t, tag="bank%d" % (PACK + t)
-            )
-            multiply(t, 0, x_codes, x_scales)
-        quantise_mean(0)
-        quantise_mean(1)
-        multiply(LAST, 1, mean_codes, mean_scales)
-        for t in range(LAST):
-            multiply(t, 1, mean_codes, mean_scales)
-        add_bias_to_x(1)
         add_bias_to_x(2)
-        finish_beside(LAST)
-        for t in range(LAST):
-            finish(t)
+        for t in range(PACK):
+            multiply(0, t, 0)
+        quantise_mean(0)
+        for t in [LAST] + list(range(LAST)):
+            multiply(0, t, 1)
+        quantise_mean(1)
+        for t in [LAST] + list(range(LAST)):
+            multiply(1, t, 0)
+            multiply(1, t, 1)
+        for n in range(BATCH):
+            finish_beside(n)
+            for t in range(LAST):
+                finish(n, t)

@@ -54,8 +54,8 @@ def tile_staticgraphmodule_s_kernel(tc, x, Wp, b, out):
         b_raw = keep.tile([P, PACK], BF16, name="b_raw")
         b_f32 = keep.tile([P, PACK], F32, name="b_f32")
         minus_b = keep.tile([P, PACK], F32, name="minus_b")
-        x_plus_b = keep.tile([P, LAST, BATCH, PIXELS], F32, name="x_plus_b")
-        relu = keep.tile([P, BATCH, PIXELS], F32, name="relu")
+        x_plus_b = keep.tile([P, PACK, BATCH, PIXELS], F32, name="x_plus_b")
+        relu = keep.tile([P, PIXELS], F32, name="relu")
         result = keep.tile([P, BATCH, PACK, PIXELS], F32, name="result")
 
         out_rows = [out[n].rearrange("(p t) h w -> p t (h w)", t=PACK) for n in range(BATCH)]
@@ -253,13 +253,10 @@ def tile_staticgraphmodule_s_kernel(tc, x, Wp, b, out):
 
         def finish_beside(n):
             nc.scalar.activation(
-                out=relu[:, n, :],
-                in_=sums[(n, LAST)][:],
-                func=RELU,
-                bias=b_f32[:, LAST : LAST + 1],
+                out=relu[:], in_=sums[(n, LAST)][:], func=RELU, bias=b_f32[:, LAST : LAST + 1]
             )
             nc.gpsimd.tensor_tensor(
-                out=result[:, n, LAST, :], in0=relu[:, n, :], in1=x_raw[:, n, LAST, :], op=ADD
+                out=result[:, n, LAST, :], in0=relu[:], in1=x_raw[:, n, LAST, :], op=ADD
             )
             nc.scalar.dma_start(out=out_rows[n][:, LAST, :], in_=result[:, n, LAST, :])
 
@@ -342,10 +339,12 @@ def tile_staticgraphmodule_s_kernel(tc, x, Wp, b, out):
         for t in [LAST] + list(range(LAST)):
             multiply(0, t, 1)
         quantise_mean(1)
-        for t in [LAST] + list(range(LAST)):
+        for t in range(PACK):
             multiply(1, t, 0)
             multiply(1, t, 1)
-        for n in range(BATCH):
-            finish_beside(n)
-            for t in range(LAST):
-                finish(n, t)
+        finish_beside(0)
+        add_bias_to_x(LAST)
+        for t in range(LAST):
+            finish(0, t)
+        for t in range(PACK):
+            finish(1, t)

@@ -8,9 +8,7 @@ U8 = mybir.dt.uint8
 FP8X4 = mybir.dt.float8_e4m3fn_x4
 ADD = mybir.AluOpType.add
 MULT = mybir.AluOpType.mult
-MAX = mybir.AluOpType.max
 COPY = mybir.ActivationFunctionType.Copy
-IDENTITY = mybir.ActivationFunctionType.Identity
 RELU = mybir.ActivationFunctionType.Relu
 
 P = 128
@@ -24,7 +22,7 @@ WORDS = CHANNELS // 2
 BLOCK_ROWS = P // SIDE
 INNER_ROWS = BLOCK_ROWS - 2
 BAND_ROWS = (SIDE - 2 * INNER_ROWS) // 2
-LAST = PACK - 1
+AHEAD = 2
 
 FLOPS = 2 * CHANNELS * (2 * CHANNELS) * (BATCH * PIXELS)
 
@@ -53,9 +51,7 @@ def tile_staticgraphmodule_s_kernel(tc, x, Wp, b, out):
         identity_f32 = keep.tile([P, P], F32, name="identity_f32")
         b_raw = keep.tile([P, PACK], BF16, name="b_raw")
         b_f32 = keep.tile([P, PACK], F32, name="b_f32")
-        minus_b = keep.tile([P, PACK], F32, name="minus_b")
-        x_plus_b = keep.tile([P, PACK, BATCH, PIXELS], F32, name="x_plus_b")
-        relu = keep.tile([P, PIXELS], F32, name="relu")
+        relu = keep.tile([P, BATCH, PACK, PIXELS], F32, name="relu")
         result = keep.tile([P, BATCH, PACK, PIXELS], F32, name="result")
 
         out_rows = [out[n].rearrange("(p t) h w -> p t (h w)", t=PACK) for n in range(BATCH)]
@@ -213,15 +209,15 @@ def tile_staticgraphmodule_s_kernel(tc, x, Wp, b, out):
                 in_=turned[:].rearrange("q s u o -> q s o u"),
             )
 
-        def quantise_weights(half):
-            words = slice(half * 4 * P, (half + 1) * 4 * P)
-            values = slice(half * 4 * P * PACK, (half + 1) * 4 * P * PACK)
+        def quantise_weights(t):
+            words = slice(t * 2 * P, (t + 1) * 2 * P)
+            values = slice(t * 2 * P * PACK, (t + 1) * 2 * P * PACK)
             quantise(w_codes[:, words], w_scales[:, words], w_grouped[:, values])
 
         def multiply(n, t, s):
             if s == 0:
                 sums[(n, t)] = psum.tile(
-                    [P, PIXELS], F32, name="sums%d%d" % (n, t), tag="bank%d" % (PACK * (1 - n) + t)
+                    [P, PIXELS], F32, name="sums%d%d" % (n, t), tag="bank%d" % (BATCH * t + n)
                 )
             codes, scales = ((x_codes, x_scales), (mean_codes, mean_scales))[s]
             columns = slice((2 * t + s) * P, (2 * t + s + 1) * P)
@@ -235,30 +231,16 @@ def tile_staticgraphmodule_s_kernel(tc, x, Wp, b, out):
                 stop=(s == 1),
             )
 
-        def add_bias_to_x(t):
+        def relu_with_bias(n, t):
             nc.scalar.activation(
-                out=x_plus_b[:, t], in_=x_raw[:, :, t, :], func=IDENTITY, bias=b_f32[:, t : t + 1]
+                out=relu[:, n, t, :], in_=sums[(n, t)][:], func=RELU, bias=b_f32[:, t : t + 1]
             )
 
-        def finish(n, t):
-            nc.vector.scalar_tensor_tensor(
-                out=result[:, n, t, :],
-                in0=sums[(n, t)][:],
-                scalar=minus_b[:, t : t + 1],
-                in1=x_plus_b[:, t, n, :],
-                op0=MAX,
-                op1=ADD,
+        def add_x_and_store(n, t):
+            nc.vector.tensor_tensor(
+                out=result[:, n, t, :], in0=relu[:, n, t, :], in1=x_raw[:, n, t, :], op=ADD
             )
             nc.sync.dma_start(out=out_rows[n][:, t, :], in_=result[:, n, t, :])
-
-        def finish_beside(n):
-            nc.scalar.activation(
-                out=relu[:], in_=sums[(n, LAST)][:], func=RELU, bias=b_f32[:, LAST : LAST + 1]
-            )
-            nc.gpsimd.tensor_tensor(
-                out=result[:, n, LAST, :], in0=relu[:], in1=x_raw[:, n, LAST, :], op=ADD
-            )
-            nc.scalar.dma_start(out=out_rows[n][:, LAST, :], in_=result[:, n, LAST, :])
 
         nc.scalar.dma_start(out=b_raw[:], in_=b.rearrange("(p t) -> p t", t=PACK))
         for n in range(BATCH):
@@ -291,13 +273,13 @@ def tile_staticgraphmodule_s_kernel(tc, x, Wp, b, out):
         add_left_and_right(unit_images)
         finish_mean(unit_images)
         nc.scalar.activation(out=b_f32[:], in_=b_raw[:], func=COPY)
-        nc.scalar.activation(out=minus_b[:], in_=b_raw[:], func=COPY, scale=-1.0)
 
         turn_x(0)
         regroup(0)
         turn_x(1)
         regroup(1)
-        add_bias_to_x(0)
+        mean_by_matrix(0)
+        mean_by_matrix(1)
         bands = [
             mean_by_adds(
                 name,
@@ -314,9 +296,6 @@ def tile_staticgraphmodule_s_kernel(tc, x, Wp, b, out):
         quantise_x(0)
         for band in bands:
             add_centre(band)
-        turn_weights(0)
-        turn_weights(1)
-        add_bias_to_x(1)
         for band in bands:
             divide_up_down(band)
         for band in bands:
@@ -324,27 +303,20 @@ def tile_staticgraphmodule_s_kernel(tc, x, Wp, b, out):
         quantise_x(1)
         for band in bands:
             add_left_and_right(band)
-        turn_weights(2)
-        turn_weights(3)
-        quantise_weights(0)
         for band in bands:
             finish_mean(band)
-        quantise_weights(1)
-        mean_by_matrix(0)
-        mean_by_matrix(1)
-        add_bias_to_x(2)
         for t in range(PACK):
-            multiply(0, t, 0)
-        quantise_mean(0)
-        for t in [LAST] + list(range(LAST)):
-            multiply(0, t, 1)
-        quantise_mean(1)
+            turn_weights(t)
+        for t in range(AHEAD):
+            quantise_weights(t)
+        for n in range(BATCH):
+            quantise_mean(n)
         for t in range(PACK):
-            multiply(1, t, 0)
-            multiply(1, t, 1)
-        finish_beside(0)
-        add_bias_to_x(LAST)
-        for t in range(LAST):
-            finish(0, t)
-        for t in range(PACK):
-            finish(1, t)
+            for n in range(BATCH):
+                multiply(n, t, 0)
+                multiply(n, t, 1)
+                relu_with_bias(n, t)
+            if t + AHEAD < PACK:
+                quantise_weights(t + AHEAD)
+            for n in range(BATCH):
+                add_x_and_store(n, t)

@@ -9,7 +9,8 @@ FP8X4 = mybir.dt.float8_e4m3fn_x4
 ADD = mybir.AluOpType.add
 MULT = mybir.AluOpType.mult
 COPY = mybir.ActivationFunctionType.Copy
-RELU = mybir.ActivationFunctionType.Relu
+IDENTITY = mybir.ActivationFunctionType.Identity
+MAX = mybir.AluOpType.max
 
 P = 128
 PACK = 4
@@ -21,7 +22,7 @@ ROW = SIDE * PACK
 WORDS = CHANNELS // 2
 BLOCK_ROWS = P // SIDE
 INNER_ROWS = BLOCK_ROWS - 2
-BAND_ROWS = (SIDE - 2 * INNER_ROWS) // 2
+BAND_ROWS = SIDE - 2 * INNER_ROWS
 AHEAD = 2
 
 FLOPS = 2 * CHANNELS * (2 * CHANNELS) * (BATCH * PIXELS)
@@ -35,9 +36,9 @@ def tile_staticgraphmodule_s_kernel(tc, x, Wp, b, out):
         tc.manual_schedule(),
     ):
         x_raw = keep.tile([P, BATCH, PACK, PIXELS], BF16, name="x_raw")
-        x_pad = keep.tile([P, BATCH, SIDE + 2, ROW], BF16, name="x_pad", align_bytes=64)
+        x_pad = keep.tile([P, BATCH, SIDE, ROW], BF16, name="x_pad", align_bytes=64)
         x_by_pixel = keep.tile([P, BATCH, 2, PACK, P], BF16, name="x_by_pixel")
-        matrix = keep.tile([P, INNER_ROWS * SIDE], BF16, name="matrix")
+        matrix = keep.tile([P, P], BF16, name="matrix")
         mean = keep.tile([P, BATCH, SIDE, ROW], BF16, name="mean", align_bytes=64)
         x_codes = keep.tile([P, BATCH, PIXELS], U32, name="x_codes", align_bytes=64)
         x_scales = keep.tile([P, BATCH, PIXELS], U8, name="x_scales", align_bytes=64)
@@ -47,11 +48,13 @@ def tile_staticgraphmodule_s_kernel(tc, x, Wp, b, out):
         w_grouped = keep.tile([P, PACK * 2 * P * PACK], BF16, name="w_grouped", align_bytes=64)
         w_codes = keep.tile([P, PACK * 2 * P], U32, name="w_codes", align_bytes=64)
         w_scales = keep.tile([P, PACK * 2 * P], U8, name="w_scales", align_bytes=64)
-        identity_bf16 = keep.tile([P, P], BF16, name="identity_bf16")
+        unit_pad = keep.tile([P, (BLOCK_ROWS + 2) * SIDE], BF16, name="unit_pad")
+        identity_bf16 = unit_pad[:, SIDE : SIDE + P]
         identity_f32 = keep.tile([P, P], F32, name="identity_f32")
         b_raw = keep.tile([P, PACK], BF16, name="b_raw")
         b_f32 = keep.tile([P, PACK], F32, name="b_f32")
-        relu = keep.tile([P, BATCH, PACK, PIXELS], F32, name="relu")
+        minus_b = keep.tile([P, PACK], F32, name="minus_b")
+        x_plus_b = keep.tile([P, BATCH, PACK, PIXELS], F32, name="x_plus_b")
         result = keep.tile([P, BATCH, PACK, PIXELS], F32, name="result")
 
         out_rows = [out[n].rearrange("(p t) h w -> p t (h w)", t=PACK) for n in range(BATCH)]
@@ -90,10 +93,15 @@ def tile_staticgraphmodule_s_kernel(tc, x, Wp, b, out):
                 op=ADD,
             )
 
-        def divide_up_down(work):
-            nc.vector.tensor_scalar_mul(
-                out=work["up_down_8th"][:], in0=work["up_down"][:], scalar1=0.125
-            )
+        def divide_up_down(work, engine):
+            if engine == "vector":
+                nc.vector.tensor_scalar_mul(
+                    out=work["up_down_8th"][:], in0=work["up_down"][:], scalar1=0.125
+                )
+            else:
+                nc.scalar.activation(
+                    out=work["up_down_8th"][:], in_=work["up_down"][:], func=COPY, scale=0.125
+                )
 
         def repeat_end_columns(work):
             pixels = work["column3"][:].rearrange("p g i (j t) -> p (g i) j t", t=work["pack"])
@@ -122,16 +130,8 @@ def tile_staticgraphmodule_s_kernel(tc, x, Wp, b, out):
 
         def regroup(n):
             nc.vector.tensor_copy(
-                out=x_pad[:, n, 1 : SIDE + 1, :].rearrange("p r (c i t) -> p (r c) t i", i=4, t=PACK),
+                out=x_pad[:, n].rearrange("p r (c i t) -> p (r c) t i", i=4, t=PACK),
                 in_=x_raw[:, n].rearrange("p t (c i) -> p c t i", i=4),
-            )
-            nc.vector.tensor_copy(
-                out=x_pad[:, n, 0 : SIDE + 2 : SIDE + 1, :].rearrange(
-                    "p e (j t) -> p e j t", t=PACK
-                ),
-                in_=x_raw[:, n]
-                .rearrange("p t (i j) -> p t i j", j=SIDE)[:, :, 0 : SIDE : SIDE - 1, :]
-                .rearrange("p t e j -> p e j t"),
             )
 
         def quantise(codes, scales, values):
@@ -141,7 +141,7 @@ def tile_staticgraphmodule_s_kernel(tc, x, Wp, b, out):
             quantise(
                 x_codes[:, n, :],
                 x_scales[:, n, :],
-                x_pad[:, n, 1 : SIDE + 1, :].rearrange("p i r -> p (i r)"),
+                x_pad[:, n].rearrange("p i r -> p (i r)"),
             )
 
         def quantise_mean(n):
@@ -151,24 +151,29 @@ def tile_staticgraphmodule_s_kernel(tc, x, Wp, b, out):
                 mean[:, n].rearrange("p i r -> p (i r)"),
             )
 
-        def turn_x(n):
+        def turn_x(n, fillers):
             for block in range(2):
+                add_b_to_x(slice(n, n + 1), fillers[block])
                 turned = psum.tile(
                     [P, PACK, P],
                     BF16,
                     name="x_turned%d%d" % (n, block),
                     tag="bank%d" % (2 * n + block),
                 )
-                first = (BAND_ROWS - 1 + block * INNER_ROWS) * SIDE
+                first = block * P
                 for t in range(PACK):
                     nc.tensor.transpose(
                         out=turned[:, t, :],
                         in_=x_raw[:, n, t, first : first + P],
-                        identity=identity_bf16[:],
+                        identity=identity_bf16,
                     )
-                nc.scalar.copy(out=x_by_pixel[:, n, block], in_=turned[:])
+                nc.scalar.copy(
+                    out=x_by_pixel[:, n, block].rearrange("k t p -> k (t p)").bitcast(F32),
+                    in_=turned[:].rearrange("k t p -> k (t p)").bitcast(F32),
+                )
 
         def mean_by_matrix(n):
+            edge = (BLOCK_ROWS - INNER_ROWS) * SIDE
             for block in range(2):
                 means = psum.tile(
                     [P, PACK, INNER_ROWS * SIDE],
@@ -180,11 +185,11 @@ def tile_staticgraphmodule_s_kernel(tc, x, Wp, b, out):
                     nc.tensor.matmul(
                         out=means[:, t, :],
                         lhsT=x_by_pixel[:, n, block, t, :],
-                        rhs=matrix[:],
+                        rhs=matrix[:, block * edge : block * edge + INNER_ROWS * SIDE],
                         start=True,
                         stop=True,
                     )
-                first_row = BAND_ROWS + block * INNER_ROWS
+                first_row = block * (INNER_ROWS + BAND_ROWS)
                 nc.scalar.copy(
                     out=mean[:, n, first_row : first_row + INNER_ROWS, :].rearrange(
                         "p i (j t) -> p (i j) t", t=PACK
@@ -231,14 +236,22 @@ def tile_staticgraphmodule_s_kernel(tc, x, Wp, b, out):
                 stop=(s == 1),
             )
 
-        def relu_with_bias(n, t):
+        def add_b_to_x(batches, t):
             nc.scalar.activation(
-                out=relu[:, n, t, :], in_=sums[(n, t)][:], func=RELU, bias=b_f32[:, t : t + 1]
+                out=x_plus_b[:, batches, t, :],
+                in_=x_raw[:, batches, t, :],
+                func=IDENTITY,
+                bias=b_f32[:, t : t + 1],
             )
 
-        def add_x_and_store(n, t):
-            nc.vector.tensor_tensor(
-                out=result[:, n, t, :], in0=relu[:, n, t, :], in1=x_raw[:, n, t, :], op=ADD
+        def finish_and_store(n, t):
+            nc.vector.scalar_tensor_tensor(
+                out=result[:, n, t, :],
+                in0=sums[(n, t)][:],
+                scalar=minus_b[:, t : t + 1],
+                in1=x_plus_b[:, n, t, :],
+                op0=MAX,
+                op1=ADD,
             )
             nc.sync.dma_start(out=out_rows[n][:, t, :], in_=result[:, n, t, :])
 
@@ -256,57 +269,56 @@ def tile_staticgraphmodule_s_kernel(tc, x, Wp, b, out):
                 in_=w_rows[:, 2 * half : 2 * half + 2, :],
             )
 
-        make_identity(nc, identity_bf16[:])
+        make_identity(nc, identity_bf16)
         make_identity(nc, identity_f32[:])
+        unit_rows = unit_pad[:].rearrange("k (i j) -> k i j", j=SIDE)
+        nc.vector.tensor_copy(
+            out=unit_rows[:, 0 : BLOCK_ROWS + 2 : BLOCK_ROWS + 1, :],
+            in_=unit_rows[:, 1 : BLOCK_ROWS + 1 : BLOCK_ROWS - 1, :],
+        )
         unit_images = mean_by_adds(
             "matrix",
-            identity_bf16[:].rearrange("k (g i j) -> k g i j", g=1, j=SIDE),
+            unit_pad[:].rearrange("k (g i j) -> k g i j", g=1, j=SIDE),
             0,
-            INNER_ROWS,
+            BLOCK_ROWS,
             1,
             matrix[:].rearrange("k (g m) -> k g m", g=1),
         )
         add_up_and_down(unit_images)
         add_centre(unit_images)
-        divide_up_down(unit_images)
+        divide_up_down(unit_images, "vector")
         repeat_end_columns(unit_images)
         add_left_and_right(unit_images)
         finish_mean(unit_images)
         nc.scalar.activation(out=b_f32[:], in_=b_raw[:], func=COPY)
+        nc.scalar.activation(out=minus_b[:], in_=b_raw[:], func=COPY, scale=-1.0)
 
-        turn_x(0)
+        turn_x(0, (0, 1))
         regroup(0)
-        turn_x(1)
+        turn_x(1, (0, 1))
         regroup(1)
+        band = mean_by_adds(
+            "band",
+            x_pad[:],
+            INNER_ROWS - 1,
+            BAND_ROWS,
+            PACK,
+            mean[:, :, INNER_ROWS : INNER_ROWS + BAND_ROWS, :].rearrange("p n i r -> p n (i r)"),
+        )
+        add_up_and_down(band)
         mean_by_matrix(0)
+        divide_up_down(band, "scalar")
         mean_by_matrix(1)
-        bands = [
-            mean_by_adds(
-                name,
-                x_pad[:],
-                first_row,
-                BAND_ROWS,
-                PACK,
-                mean[:, :, first_row : first_row + BAND_ROWS, :].rearrange("p n i r -> p n (i r)"),
-            )
-            for name, first_row in (("top", 0), ("bottom", SIDE - BAND_ROWS))
-        ]
-        for band in bands:
-            add_up_and_down(band)
         quantise_x(0)
-        for band in bands:
-            add_centre(band)
-        for band in bands:
-            divide_up_down(band)
-        for band in bands:
-            repeat_end_columns(band)
+        add_centre(band)
         quantise_x(1)
-        for band in bands:
-            add_left_and_right(band)
-        for band in bands:
-            finish_mean(band)
+        repeat_end_columns(band)
+        add_left_and_right(band)
+        finish_mean(band)
         for t in range(PACK):
             turn_weights(t)
+        for t in range(AHEAD, PACK):
+            add_b_to_x(slice(0, BATCH), t)
         for t in range(AHEAD):
             quantise_weights(t)
         for n in range(BATCH):
@@ -315,8 +327,7 @@ def tile_staticgraphmodule_s_kernel(tc, x, Wp, b, out):
             for n in range(BATCH):
                 multiply(n, t, 0)
                 multiply(n, t, 1)
-                relu_with_bias(n, t)
             if t + AHEAD < PACK:
                 quantise_weights(t + AHEAD)
             for n in range(BATCH):
-                add_x_and_store(n, t)
+                finish_and_store(n, t)

@@ -79,17 +79,17 @@ def tile_staticgraphmodule_s_kernel(tc, x, Wp, b, out):
                 "sides": keep.tile(shape, F32, name=name + "_sides"),
             }
 
-        def add_up_and_down(work):
+        def add_up_and_down(work, g):
             nc.vector.tensor_tensor(
-                out=work["up_down"][:], in0=work["above"], in1=work["below"], op=ADD
+                out=work["up_down"][:, g], in0=work["above"][:, g], in1=work["below"][:, g], op=ADD
             )
 
-        def add_centre(work):
+        def add_centre(work, g):
             pack = work["pack"]
             nc.vector.tensor_tensor(
-                out=work["column3"][:, :, :, pack : pack + work["width"]],
-                in0=work["up_down"][:],
-                in1=work["centre"],
+                out=work["column3"][:, g, :, pack : pack + work["width"]],
+                in0=work["up_down"][:, g],
+                in1=work["centre"][:, g],
                 op=ADD,
             )
 
@@ -103,27 +103,27 @@ def tile_staticgraphmodule_s_kernel(tc, x, Wp, b, out):
                     out=work["up_down_8th"][:], in_=work["up_down"][:], func=COPY, scale=0.125
                 )
 
-        def repeat_end_columns(work):
-            pixels = work["column3"][:].rearrange("p g i (j t) -> p (g i) j t", t=work["pack"])
+        def repeat_end_columns(work, g):
+            pixels = work["column3"][:, g].rearrange("p g i (j t) -> p (g i) j t", t=work["pack"])
             nc.vector.tensor_copy(
                 out=pixels[:, :, 0 : SIDE + 2 : SIDE + 1, :],
                 in_=pixels[:, :, 1 : SIDE + 1 : SIDE - 1, :],
             )
 
-        def add_left_and_right(work):
+        def add_left_and_right(work, g):
             nc.vector.tensor_tensor(
-                out=work["sides"][:],
-                in0=work["column3"][:, :, :, 0 : work["width"]],
-                in1=work["column3"][:, :, :, 2 * work["pack"] : 2 * work["pack"] + work["width"]],
+                out=work["sides"][:, g],
+                in0=work["column3"][:, g, :, 0 : work["width"]],
+                in1=work["column3"][:, g, :, 2 * work["pack"] : 2 * work["pack"] + work["width"]],
                 op=ADD,
             )
 
-        def finish_mean(work):
+        def finish_mean(work, g):
             nc.vector.scalar_tensor_tensor(
-                out=work["target"],
-                in0=work["sides"][:].rearrange("p g i r -> p g (i r)"),
+                out=work["target"][:, g],
+                in0=work["sides"][:, g].rearrange("p g i r -> p g (i r)"),
                 scalar=0.125,
-                in1=work["up_down_8th"][:].rearrange("p g i r -> p g (i r)"),
+                in1=work["up_down_8th"][:, g].rearrange("p g i r -> p g (i r)"),
                 op0=MULT,
                 op1=ADD,
             )
@@ -284,12 +284,13 @@ def tile_staticgraphmodule_s_kernel(tc, x, Wp, b, out):
             1,
             matrix[:].rearrange("k (g m) -> k g m", g=1),
         )
-        add_up_and_down(unit_images)
-        add_centre(unit_images)
+        whole = slice(0, 1)
+        add_up_and_down(unit_images, whole)
+        add_centre(unit_images, whole)
         divide_up_down(unit_images, "vector")
-        repeat_end_columns(unit_images)
-        add_left_and_right(unit_images)
-        finish_mean(unit_images)
+        repeat_end_columns(unit_images, whole)
+        add_left_and_right(unit_images, whole)
+        finish_mean(unit_images, whole)
         nc.scalar.activation(out=b_f32[:], in_=b_raw[:], func=COPY)
         nc.scalar.activation(out=minus_b[:], in_=b_raw[:], func=COPY, scale=-1.0)
 
@@ -305,16 +306,22 @@ def tile_staticgraphmodule_s_kernel(tc, x, Wp, b, out):
             PACK,
             mean[:, :, INNER_ROWS : INNER_ROWS + BAND_ROWS, :].rearrange("p n i r -> p n (i r)"),
         )
-        add_up_and_down(band)
+        first, second = slice(0, 1), slice(1, 2)
+        add_up_and_down(band, first)
+        quantise_x(0)
+        add_up_and_down(band, second)
         mean_by_matrix(0)
         divide_up_down(band, "scalar")
         mean_by_matrix(1)
-        quantise_x(0)
-        add_centre(band)
+        add_centre(band, first)
         quantise_x(1)
-        repeat_end_columns(band)
-        add_left_and_right(band)
-        finish_mean(band)
+        add_centre(band, second)
+        repeat_end_columns(band, first)
+        repeat_end_columns(band, second)
+        add_left_and_right(band, first)
+        add_left_and_right(band, second)
+        finish_mean(band, first)
+        finish_mean(band, second)
         for t in range(PACK):
             turn_weights(t)
         for t in range(AHEAD, PACK):

@@ -9,8 +9,7 @@ FP8X4 = mybir.dt.float8_e4m3fn_x4
 ADD = mybir.AluOpType.add
 MULT = mybir.AluOpType.mult
 COPY = mybir.ActivationFunctionType.Copy
-IDENTITY = mybir.ActivationFunctionType.Identity
-MAX = mybir.AluOpType.max
+RELU = mybir.ActivationFunctionType.Relu
 
 P = 128
 PACK = 4
@@ -53,8 +52,7 @@ def tile_staticgraphmodule_s_kernel(tc, x, Wp, b, out):
         identity_f32 = keep.tile([P, P], F32, name="identity_f32")
         b_raw = keep.tile([P, PACK], BF16, name="b_raw")
         b_f32 = keep.tile([P, PACK], F32, name="b_f32")
-        minus_b = keep.tile([P, PACK], F32, name="minus_b")
-        x_plus_b = keep.tile([P, BATCH, PACK, PIXELS], F32, name="x_plus_b")
+        relu = keep.tile([P, BATCH, PACK, PIXELS], F32, name="relu")
         result = keep.tile([P, BATCH, PACK, PIXELS], F32, name="result")
 
         out_rows = [out[n].rearrange("(p t) h w -> p t (h w)", t=PACK) for n in range(BATCH)]
@@ -93,15 +91,10 @@ def tile_staticgraphmodule_s_kernel(tc, x, Wp, b, out):
                 op=ADD,
             )
 
-        def divide_up_down(work, engine):
-            if engine == "vector":
-                nc.vector.tensor_scalar_mul(
-                    out=work["up_down_8th"][:], in0=work["up_down"][:], scalar1=0.125
-                )
-            else:
-                nc.scalar.activation(
-                    out=work["up_down_8th"][:], in_=work["up_down"][:], func=COPY, scale=0.125
-                )
+        def divide_up_down(work, g):
+            nc.vector.tensor_scalar_mul(
+                out=work["up_down_8th"][:, g], in0=work["up_down"][:, g], scalar1=0.125
+            )
 
         def repeat_end_columns(work, g):
             pixels = work["column3"][:, g].rearrange("p g i (j t) -> p (g i) j t", t=work["pack"])
@@ -151,9 +144,8 @@ def tile_staticgraphmodule_s_kernel(tc, x, Wp, b, out):
                 mean[:, n].rearrange("p i r -> p (i r)"),
             )
 
-        def turn_x(n, fillers):
+        def turn_x(n):
             for block in range(2):
-                add_b_to_x(slice(n, n + 1), fillers[block])
                 turned = psum.tile(
                     [P, PACK, P],
                     BF16,
@@ -236,22 +228,14 @@ def tile_staticgraphmodule_s_kernel(tc, x, Wp, b, out):
                 stop=(s == 1),
             )
 
-        def add_b_to_x(batches, t):
+        def relu_with_bias(n, t):
             nc.scalar.activation(
-                out=x_plus_b[:, batches, t, :],
-                in_=x_raw[:, batches, t, :],
-                func=IDENTITY,
-                bias=b_f32[:, t : t + 1],
+                out=relu[:, n, t, :], in_=sums[(n, t)][:], func=RELU, bias=b_f32[:, t : t + 1]
             )
 
-        def finish_and_store(n, t):
-            nc.vector.scalar_tensor_tensor(
-                out=result[:, n, t, :],
-                in0=sums[(n, t)][:],
-                scalar=minus_b[:, t : t + 1],
-                in1=x_plus_b[:, n, t, :],
-                op0=MAX,
-                op1=ADD,
+        def add_x_and_store(n, t):
+            nc.vector.tensor_tensor(
+                out=result[:, n, t, :], in0=relu[:, n, t, :], in1=x_raw[:, n, t, :], op=ADD
             )
             nc.sync.dma_start(out=out_rows[n][:, t, :], in_=result[:, n, t, :])
 
@@ -287,17 +271,18 @@ def tile_staticgraphmodule_s_kernel(tc, x, Wp, b, out):
         whole = slice(0, 1)
         add_up_and_down(unit_images, whole)
         add_centre(unit_images, whole)
-        divide_up_down(unit_images, "vector")
+        divide_up_down(unit_images, whole)
         repeat_end_columns(unit_images, whole)
         add_left_and_right(unit_images, whole)
         finish_mean(unit_images, whole)
         nc.scalar.activation(out=b_f32[:], in_=b_raw[:], func=COPY)
-        nc.scalar.activation(out=minus_b[:], in_=b_raw[:], func=COPY, scale=-1.0)
 
-        turn_x(0, (0, 1))
+        turn_x(0)
         regroup(0)
-        turn_x(1, (0, 1))
+        turn_x(1)
         regroup(1)
+        mean_by_matrix(0)
+        mean_by_matrix(1)
         band = mean_by_adds(
             "band",
             x_pad[:],
@@ -310,12 +295,11 @@ def tile_staticgraphmodule_s_kernel(tc, x, Wp, b, out):
         add_up_and_down(band, first)
         quantise_x(0)
         add_up_and_down(band, second)
-        mean_by_matrix(0)
-        divide_up_down(band, "scalar")
-        mean_by_matrix(1)
         add_centre(band, first)
         quantise_x(1)
         add_centre(band, second)
+        divide_up_down(band, first)
+        divide_up_down(band, second)
         repeat_end_columns(band, first)
         repeat_end_columns(band, second)
         add_left_and_right(band, first)
@@ -324,17 +308,15 @@ def tile_staticgraphmodule_s_kernel(tc, x, Wp, b, out):
         finish_mean(band, second)
         for t in range(PACK):
             turn_weights(t)
-        for t in range(AHEAD, PACK):
-            add_b_to_x(slice(0, BATCH), t)
-        for t in range(AHEAD):
+        quantise_mean(0)
+        quantise_weights(0)
+        quantise_mean(1)
+        for t in range(1, PACK):
             quantise_weights(t)
-        for n in range(BATCH):
-            quantise_mean(n)
         for t in range(PACK):
             for n in range(BATCH):
                 multiply(n, t, 0)
                 multiply(n, t, 1)
-            if t + AHEAD < PACK:
-                quantise_weights(t + AHEAD)
+                relu_with_bias(n, t)
             for n in range(BATCH):
-                finish_and_store(n, t)
+                add_x_and_store(n, t)

@@ -22,7 +22,7 @@ WORDS = CHANNELS // 2
 BLOCK_ROWS = P // SIDE
 INNER_ROWS = BLOCK_ROWS - 2
 BAND_ROWS = SIDE - 2 * INNER_ROWS
-AHEAD = 2
+WARM_PASSES = 4
 
 FLOPS = 2 * CHANNELS * (2 * CHANNELS) * (BATCH * PIXELS)
 
@@ -308,6 +308,17 @@ def tile_staticgraphmodule_s_kernel(tc, x, Wp, b, out):
         finish_mean(band, second)
         for t in range(PACK):
             turn_weights(t)
+        idle_sums = psum.tile([P, PIXELS], F32, name="idle_sums", tag="bank3")
+        for i in range(WARM_PASSES):
+            nc.tensor.matmul_mx(
+                out=idle_sums[:],
+                lhsT=x_codes[:, 0, 0:P].bitcast(FP8X4),
+                lhsT_scale=x_scales[:, 0, 0:P],
+                rhs=x_codes[:, 0, :].bitcast(FP8X4),
+                rhs_scale=x_scales[:, 0, :],
+                start=True,
+                stop=True,
+            )
         quantise_mean(0)
         quantise_weights(0)
         quantise_mean(1)

@@ -245,12 +245,9 @@ def tile_staticgraphmodule_s_kernel(tc, x, Wp, b, out):
                 out=x_raw[:, n], in_=x[n].rearrange("(p t) h w -> p t (h w)", t=PACK)
             )
         w_rows = Wp.rearrange("(p t) k -> p t k", t=PACK)
-        for half in range(2):
+        for t in range(PACK):
             nc.sync.dma_start(
-                out=w_raw[:, half * 4 * CHANNELS : (half + 1) * 4 * CHANNELS].rearrange(
-                    "p (t k) -> p t k", t=2
-                ),
-                in_=w_rows[:, 2 * half : 2 * half + 2, :],
+                out=w_raw[:, t * 2 * CHANNELS : (t + 1) * 2 * CHANNELS], in_=w_rows[:, t, :]
             )
 
         make_identity(nc, identity_bf16)

@@ -22,6 +22,7 @@ WORDS = CHANNELS // 2
 BLOCK_ROWS = P // SIDE
 INNER_ROWS = BLOCK_ROWS - 2
 BAND_ROWS = SIDE - 2 * INNER_ROWS
+HEAD_PASSES = 12
 WARM_PASSES = 4
 
 FLOPS = 2 * CHANNELS * (2 * CHANNELS) * (BATCH * PIXELS)
@@ -54,13 +55,19 @@ def tile_staticgraphmodule_s_kernel(tc, x, Wp, b, out):
         b_f32 = keep.tile([P, PACK], F32, name="b_f32")
         relu = keep.tile([P, BATCH, PACK, PIXELS], F32, name="relu")
         result = keep.tile([P, BATCH, PACK, PIXELS], F32, name="result")
+        head_values = keep.tile([P, P * PACK], BF16, name="head_values", align_bytes=64)
+        head_codes = keep.tile([P, P], U32, name="head_codes", align_bytes=64)
+        head_scales = keep.tile([P, P], U8, name="head_scales", align_bytes=64)
 
-        out_rows = [out[n].rearrange("(p t) h w -> p t (h w)", t=PACK) for n in range(BATCH)]
+        out_rows = [
+            out[n].rearrange("(u p e) h w -> p u e (h w)", u=2, e=2) for n in range(BATCH)
+        ]
         w_words = w_raw[:].bitcast(F32)
         w_grouped_words = w_grouped[:].bitcast(F32)
         sums = {}
+        matrix_rows = ((INNER_ROWS + 1, INNER_ROWS), (INNER_ROWS, INNER_ROWS))
 
-        def mean_by_adds(name, images, first_row, rows, pack, target):
+        def mean_by_adds(name, images, first_row, rows, pack, target, dtype):
             groups = images.shape[1]
             width = SIDE * pack
             shape = [P, groups, rows, width]
@@ -71,10 +78,10 @@ def tile_staticgraphmodule_s_kernel(tc, x, Wp, b, out):
                 "target": target,
                 "pack": pack,
                 "width": width,
-                "up_down": keep.tile(shape, F32, name=name + "_up_down"),
-                "up_down_8th": keep.tile(shape, F32, name=name + "_up_down_8th"),
-                "column3": keep.tile([P, groups, rows, width + 2 * pack], F32, name=name + "_column3"),
-                "sides": keep.tile(shape, F32, name=name + "_sides"),
+                "up_down": keep.tile(shape, dtype, name=name + "_up_down"),
+                "up_down_8th": keep.tile(shape, dtype, name=name + "_up_down_8th"),
+                "column3": keep.tile([P, groups, rows, width + 2 * pack], dtype, name=name + "_column3"),
+                "sides": keep.tile(shape, dtype, name=name + "_sides"),
             }
 
         def add_up_and_down(work, g):
@@ -165,10 +172,11 @@ def tile_staticgraphmodule_s_kernel(tc, x, Wp, b, out):
                 )
 
         def mean_by_matrix(n):
-            edge = (BLOCK_ROWS - INNER_ROWS) * SIDE
             for block in range(2):
+                rows = matrix_rows[n][block]
+                first_column = block * (BLOCK_ROWS - rows) * SIDE
                 means = psum.tile(
-                    [P, PACK, INNER_ROWS * SIDE],
+                    [P, PACK, rows * SIDE],
                     F32,
                     name="means%d%d" % (n, block),
                     tag="bank%d" % (2 * n + block),
@@ -177,13 +185,13 @@ def tile_staticgraphmodule_s_kernel(tc, x, Wp, b, out):
                     nc.tensor.matmul(
                         out=means[:, t, :],
                         lhsT=x_by_pixel[:, n, block, t, :],
-                        rhs=matrix[:, block * edge : block * edge + INNER_ROWS * SIDE],
+                        rhs=matrix[:, first_column : first_column + rows * SIDE],
                         start=True,
                         stop=True,
                     )
-                first_row = block * (INNER_ROWS + BAND_ROWS)
+                first_row = block * (SIDE - rows)
                 nc.scalar.copy(
-                    out=mean[:, n, first_row : first_row + INNER_ROWS, :].rearrange(
+                    out=mean[:, n, first_row : first_row + rows, :].rearrange(
                         "p i (j t) -> p (i j) t", t=PACK
                     ),
                     in_=means[:].rearrange("p t m -> p m t"),
@@ -193,10 +201,10 @@ def tile_staticgraphmodule_s_kernel(tc, x, Wp, b, out):
             turned = psum.tile([P, 2, 2, P], F32, name="w_turned%d" % t, tag="bank%d" % (PACK + t))
             for s in range(2):
                 for u in range(2):
-                    first = (2 * t + s) * WORDS + u
+                    first = (2 * t + s) * WORDS + u * P
                     nc.tensor.transpose(
                         out=turned[:, s, u, :],
-                        in_=w_words[:, first : (2 * t + s + 1) * WORDS : 2],
+                        in_=w_words[:, first : first + P],
                         identity=identity_f32[:],
                     )
             nc.scalar.copy(
@@ -237,17 +245,36 @@ def tile_staticgraphmodule_s_kernel(tc, x, Wp, b, out):
             nc.vector.tensor_tensor(
                 out=result[:, n, t, :], in0=relu[:, n, t, :], in1=x_raw[:, n, t, :], op=ADD
             )
-            nc.sync.dma_start(out=out_rows[n][:, t, :], in_=result[:, n, t, :])
+            nc.sync.dma_start(out=out_rows[n][:, t // 2, t % 2, :], in_=result[:, n, t, :])
 
-        nc.scalar.dma_start(out=b_raw[:], in_=b.rearrange("(p t) -> p t", t=PACK))
+        nc.scalar.dma_start(
+            out=b_raw[:].rearrange("p (u e) -> p u e", u=2),
+            in_=b.rearrange("(u p e) -> p u e", u=2, e=2),
+        )
         for n in range(BATCH):
             nc.sync.dma_start(
-                out=x_raw[:, n], in_=x[n].rearrange("(p t) h w -> p t (h w)", t=PACK)
+                out=x_raw[:, n].rearrange("p (u e) m -> p u (e m)", u=2),
+                in_=x[n].rearrange("(u p e) h w -> p u (e h w)", u=2, e=2),
             )
-        w_rows = Wp.rearrange("(p t) k -> p t k", t=PACK)
+        w_rows = Wp.rearrange("(u p e) k -> p u e k", u=2, e=2)
         for t in range(PACK):
             nc.sync.dma_start(
-                out=w_raw[:, t * 2 * CHANNELS : (t + 1) * 2 * CHANNELS], in_=w_rows[:, t, :]
+                out=w_raw[:, t * 2 * CHANNELS : (t + 1) * 2 * CHANNELS],
+                in_=w_rows[:, t // 2, t % 2, :],
+            )
+
+        nc.vector.memset(head_values[:].bitcast(F32), 1.0)
+        quantise(head_codes[:], head_scales[:], head_values[:])
+        head_sums = psum.tile([P, P], F32, name="head_sums", tag="bank7")
+        for i in range(HEAD_PASSES):
+            nc.tensor.matmul_mx(
+                out=head_sums[:],
+                lhsT=head_codes[:].bitcast(FP8X4),
+                lhsT_scale=head_scales[:],
+                rhs=head_codes[:].bitcast(FP8X4),
+                rhs_scale=head_scales[:],
+                start=True,
+                stop=True,
             )
 
         make_identity(nc, identity_bf16)
@@ -264,6 +291,7 @@ def tile_staticgraphmodule_s_kernel(tc, x, Wp, b, out):
             BLOCK_ROWS,
             1,
             matrix[:].rearrange("k (g m) -> k g m", g=1),
+            BF16,
         )
         whole = slice(0, 1)
         add_up_and_down(unit_images, whole)
@@ -280,29 +308,34 @@ def tile_staticgraphmodule_s_kernel(tc, x, Wp, b, out):
         regroup(1)
         mean_by_matrix(0)
         mean_by_matrix(1)
-        band = mean_by_adds(
-            "band",
-            x_pad[:],
-            INNER_ROWS - 1,
-            BAND_ROWS,
-            PACK,
-            mean[:, :, INNER_ROWS : INNER_ROWS + BAND_ROWS, :].rearrange("p n i r -> p n (i r)"),
-        )
-        first, second = slice(0, 1), slice(1, 2)
-        add_up_and_down(band, first)
+        bands = []
+        for n in range(BATCH):
+            top, bottom = matrix_rows[n]
+            bands.append(
+                mean_by_adds(
+                    "band%d" % n,
+                    x_pad[:, n : n + 1],
+                    top - 1,
+                    SIDE - top - bottom,
+                    PACK,
+                    mean[:, n : n + 1, top : SIDE - bottom, :].rearrange("p n i r -> p n (i r)"),
+                    F32,
+                )
+            )
+        add_up_and_down(bands[0], whole)
         quantise_x(0)
-        add_up_and_down(band, second)
-        add_centre(band, first)
+        add_up_and_down(bands[1], whole)
+        add_centre(bands[0], whole)
         quantise_x(1)
-        add_centre(band, second)
-        divide_up_down(band, first)
-        divide_up_down(band, second)
-        repeat_end_columns(band, first)
-        repeat_end_columns(band, second)
-        add_left_and_right(band, first)
-        add_left_and_right(band, second)
-        finish_mean(band, first)
-        finish_mean(band, second)
+        add_centre(bands[1], whole)
+        for step in (
+            divide_up_down,
+            repeat_end_columns,
+            add_left_and_right,
+            finish_mean,
+        ):
+            for band in bands:
+                step(band, whole)
         for t in range(PACK):
             turn_weights(t)
         idle_sums = psum.tile([P, PIXELS], F32, name="idle_sums", tag="bank3")

import concourse.mybir as mybir
from concourse.masks import make_identity

F32 = mybir.dt.float32
BF16 = mybir.dt.bfloat16
U32 = mybir.dt.uint32
U8 = mybir.dt.uint8
FP8X4 = mybir.dt.float8_e4m3fn_x4
ADD = mybir.AluOpType.add
MULT = mybir.AluOpType.mult
COPY = mybir.ActivationFunctionType.Copy
RELU = mybir.ActivationFunctionType.Relu

P = 128
PACK = 4
BATCH = 2
CHANNELS = P * PACK
SIDE = 16
PIXELS = SIDE * SIDE
ROW = SIDE * PACK
WORDS = CHANNELS // 2
BLOCK_ROWS = P // SIDE
INNER_ROWS = BLOCK_ROWS - 2
BAND_ROWS = SIDE - 2 * INNER_ROWS
HEAD_PASSES = 12
WARM_PASSES = 4

FLOPS = 2 * CHANNELS * (2 * CHANNELS) * (BATCH * PIXELS)


def tile_staticgraphmodule_s_kernel(tc, x, Wp, b, out):
    nc = tc.nc
    with (
        tc.tile_pool(name="keep", bufs=1) as keep,
        tc.psum_pool(name="psum", bufs=1) as psum,
        tc.manual_schedule(),
    ):
        x_raw = keep.tile([P, BATCH, PACK, PIXELS], BF16, name="x_raw")
        x_pad = keep.tile([P, BATCH, SIDE, ROW], BF16, name="x_pad", align_bytes=64)
        x_by_pixel = keep.tile([P, BATCH, 2, PACK, P], BF16, name="x_by_pixel")
        matrix = keep.tile([P, P], BF16, name="matrix")
        mean = keep.tile([P, BATCH, SIDE, ROW], BF16, name="mean", align_bytes=64)
        x_codes = keep.tile([P, BATCH, PIXELS], U32, name="x_codes", align_bytes=64)
        x_scales = keep.tile([P, BATCH, PIXELS], U8, name="x_scales", align_bytes=64)
        mean_codes = keep.tile([P, BATCH, PIXELS], U32, name="mean_codes", align_bytes=64)
        mean_scales = keep.tile([P, BATCH, PIXELS], U8, name="mean_scales", align_bytes=64)
        w_raw = keep.tile([P, PACK * 2 * CHANNELS], BF16, name="w_raw")
        w_grouped = keep.tile([P, PACK * 2 * P * PACK], BF16, name="w_grouped", align_bytes=64)
        w_codes = keep.tile([P, PACK * 2 * P], U32, name="w_codes", align_bytes=64)
        w_scales = keep.tile([P, PACK * 2 * P], U8, name="w_scales", align_bytes=64)
        unit_pad = keep.tile([P, (BLOCK_ROWS + 2) * SIDE], BF16, name="unit_pad")
        identity_bf16 = unit_pad[:, SIDE : SIDE + P]
        identity_f32 = keep.tile([P, P], F32, name="identity_f32")
        b_raw = keep.tile([P, PACK], BF16, name="b_raw")
        b_f32 = keep.tile([P, PACK], F32, name="b_f32")
        relu = keep.tile([P, BATCH, PACK, PIXELS], F32, name="relu")
        result = keep.tile([P, BATCH, PACK, PIXELS], F32, name="result")
        head_values = keep.tile([P, P * PACK], BF16, name="head_values", align_bytes=64)
        head_codes = keep.tile([P, P], U32, name="head_codes", align_bytes=64)
        head_scales = keep.tile([P, P], U8, name="head_scales", align_bytes=64)

        out_rows = [
            out[n].rearrange("(u p e) h w -> p u e (h w)", u=2, e=2) for n in range(BATCH)
        ]
        w_words = w_raw[:].bitcast(F32)
        w_grouped_words = w_grouped[:].bitcast(F32)
        sums = {}
        matrix_rows = ((INNER_ROWS + 1, INNER_ROWS), (INNER_ROWS, INNER_ROWS))

        def mean_by_adds(name, images, first_row, rows, pack, target, dtype):
            groups = images.shape[1]
            width = SIDE * pack
            shape = [P, groups, rows, width]
            return {
                "above": images[:, :, first_row : first_row + rows, :],
                "centre": images[:, :, first_row + 1 : first_row + 1 + rows, :],
                "below": images[:, :, first_row + 2 : first_row + 2 + rows, :],
                "target": target,
                "pack": pack,
                "width": width,
                "up_down": keep.tile(shape, dtype, name=name + "_up_down"),
                "up_down_8th": keep.tile(shape, dtype, name=name + "_up_down_8th"),
                "column3": keep.tile([P, groups, rows, width + 2 * pack], dtype, name=name + "_column3"),
                "sides": keep.tile(shape, dtype, name=name + "_sides"),
            }

        def add_up_and_down(work, g):
            nc.vector.tensor_tensor(
                out=work["up_down"][:, g], in0=work["above"][:, g], in1=work["below"][:, g], op=ADD
            )

        def add_centre(work, g):
            pack = work["pack"]
            nc.vector.tensor_tensor(
                out=work["column3"][:, g, :, pack : pack + work["width"]],
                in0=work["up_down"][:, g],
                in1=work["centre"][:, g],
                op=ADD,
            )

        def divide_up_down(work, g):
            nc.vector.tensor_scalar_mul(
                out=work["up_down_8th"][:, g], in0=work["up_down"][:, g], scalar1=0.125
            )

        def repeat_end_columns(work, g):
            pixels = work["column3"][:, g].rearrange("p g i (j t) -> p (g i) j t", t=work["pack"])
            nc.vector.tensor_copy(
                out=pixels[:, :, 0 : SIDE + 2 : SIDE + 1, :],
                in_=pixels[:, :, 1 : SIDE + 1 : SIDE - 1, :],
            )

        def add_left_and_right(work, g):
            nc.vector.tensor_tensor(
                out=work["sides"][:, g],
                in0=work["column3"][:, g, :, 0 : work["width"]],
                in1=work["column3"][:, g, :, 2 * work["pack"] : 2 * work["pack"] + work["width"]],
                op=ADD,
            )

        def finish_mean(work, g):
            nc.vector.scalar_tensor_tensor(
                out=work["target"][:, g],
                in0=work["sides"][:, g].rearrange("p g i r -> p g (i r)"),
                scalar=0.125,
                in1=work["up_down_8th"][:, g].rearrange("p g i r -> p g (i r)"),
                op0=MULT,
                op1=ADD,
            )

        def regroup(n):
            nc.vector.tensor_copy(
                out=x_pad[:, n].rearrange("p r (c i t) -> p (r c) t i", i=4, t=PACK),
                in_=x_raw[:, n].rearrange("p t (c i) -> p c t i", i=4),
            )

        def quantise(codes, scales, values):
            nc.vector.quantize_mx(out=codes.bitcast(FP8X4), scales=scales, in_=values)

        def quantise_x(n):
            quantise(
                x_codes[:, n, :],
                x_scales[:, n, :],
                x_pad[:, n].rearrange("p i r -> p (i r)"),
            )

        def quantise_mean(n):
            quantise(
                mean_codes[:, n, :],
                mean_scales[:, n, :],
                mean[:, n].rearrange("p i r -> p (i r)"),
            )

        def turn_x(n):
            for block in range(2):
                turned = psum.tile(
                    [P, PACK, P],
                    BF16,
                    name="x_turned%d%d" % (n, block),
                    tag="bank%d" % (2 * n + block),
                )
                first = block * P
                for t in range(PACK):
                    nc.tensor.transpose(
                        out=turned[:, t, :],
                        in_=x_raw[:, n, t, first : first + P],
                        identity=identity_bf16,
                    )
                nc.scalar.copy(
                    out=x_by_pixel[:, n, block].rearrange("k t p -> k (t p)").bitcast(F32),
                    in_=turned[:].rearrange("k t p -> k (t p)").bitcast(F32),
                )

        def mean_by_matrix(n):
            for block in range(2):
                rows = matrix_rows[n][block]
                first_column = block * (BLOCK_ROWS - rows) * SIDE
                means = psum.tile(
                    [P, PACK, rows * SIDE],
                    F32,
                    name="means%d%d" % (n, block),
                    tag="bank%d" % (2 * n + block),
                )
                for t in range(PACK):
                    nc.tensor.matmul(
                        out=means[:, t, :],
                        lhsT=x_by_pixel[:, n, block, t, :],
                        rhs=matrix[:, first_column : first_column + rows * SIDE],
                        start=True,
                        stop=True,
                    )
                first_row = block * (SIDE - rows)
                nc.scalar.copy(
                    out=mean[:, n, first_row : first_row + rows, :].rearrange(
                        "p i (j t) -> p (i j) t", t=PACK
                    ),
                    in_=means[:].rearrange("p t m -> p m t"),
                )

        def turn_weights(t):
            turned = psum.tile([P, 2, 2, P], F32, name="w_turned%d" % t, tag="bank%d" % (PACK + t))
            for s in range(2):
                for u in range(2):
                    first = (2 * t + s) * WORDS + u * P
                    nc.tensor.transpose(
                        out=turned[:, s, u, :],
                        in_=w_words[:, first : first + P],
                        identity=identity_f32[:],
                    )
            nc.scalar.copy(
                out=w_grouped_words[:, 2 * t * WORDS : 2 * (t + 1) * WORDS].rearrange(
                    "q (s o u) -> q s o u", s=2, u=2
                ),
                in_=turned[:].rearrange("q s u o -> q s o u"),
            )

        def quantise_weights(t):
            words = slice(t * 2 * P, (t + 1) * 2 * P)
            values = slice(t * 2 * P * PACK, (t + 1) * 2 * P * PACK)
            quantise(w_codes[:, words], w_scales[:, words], w_grouped[:, values])

        def multiply(n, t, s):
            if s == 0:
                sums[(n, t)] = psum.tile(
                    [P, PIXELS], F32, name="sums%d%d" % (n, t), tag="bank%d" % (BATCH * t + n)
                )
            codes, scales = ((x_codes, x_scales), (mean_codes, mean_scales))[s]
            columns = slice((2 * t + s) * P, (2 * t + s + 1) * P)
            nc.tensor.matmul_mx(
                out=sums[(n, t)][:],
                lhsT=w_codes[:, columns].bitcast(FP8X4),
                lhsT_scale=w_scales[:, columns],
                rhs=codes[:, n, :].bitcast(FP8X4),
                rhs_scale=scales[:, n, :],
                start=(s == 0),
                stop=(s == 1),
            )

        def relu_with_bias(n, t):
            nc.scalar.activation(
                out=relu[:, n, t, :], in_=sums[(n, t)][:], func=RELU, bias=b_f32[:, t : t + 1]
            )

        def add_x_and_store(n, t):
            nc.vector.tensor_tensor(
                out=result[:, n, t, :], in0=relu[:, n, t, :], in1=x_raw[:, n, t, :], op=ADD
            )
            nc.sync.dma_start(out=out_rows[n][:, t // 2, t % 2, :], in_=result[:, n, t, :])

        nc.scalar.dma_start(
            out=b_raw[:].rearrange("p (u e) -> p u e", u=2),
            in_=b.rearrange("(u p e) -> p u e", u=2, e=2),
        )
        for n in range(BATCH):
            nc.sync.dma_start(
                out=x_raw[:, n].rearrange("p (u e) m -> p u (e m)", u=2),
                in_=x[n].rearrange("(u p e) h w -> p u (e h w)", u=2, e=2),
            )
        w_rows = Wp.rearrange("(u p e) k -> p u e k", u=2, e=2)
        for t in range(PACK):
            nc.sync.dma_start(
                out=w_raw[:, t * 2 * CHANNELS : (t + 1) * 2 * CHANNELS],
                in_=w_rows[:, t // 2, t % 2, :],
            )

        nc.vector.memset(head_values[:].bitcast(F32), 1.0)
        quantise(head_codes[:], head_scales[:], head_values[:])
        head_sums = psum.tile([P, P], F32, name="head_sums", tag="bank7")
        for i in range(HEAD_PASSES):
            nc.tensor.matmul_mx(
                out=head_sums[:],
                lhsT=head_codes[:].bitcast(FP8X4),
                lhsT_scale=head_scales[:],
                rhs=head_codes[:].bitcast(FP8X4),
                rhs_scale=head_scales[:],
                start=True,
                stop=True,
            )

        make_identity(nc, identity_bf16)
        make_identity(nc, identity_f32[:])
        unit_rows = unit_pad[:].rearrange("k (i j) -> k i j", j=SIDE)
        nc.vector.tensor_copy(
            out=unit_rows[:, 0 : BLOCK_ROWS + 2 : BLOCK_ROWS + 1, :],
            in_=unit_rows[:, 1 : BLOCK_ROWS + 1 : BLOCK_ROWS - 1, :],
        )
        unit_images = mean_by_adds(
            "matrix",
            unit_pad[:].rearrange("k (g i j) -> k g i j", g=1, j=SIDE),
            0,
            BLOCK_ROWS,
            1,
            matrix[:].rearrange("k (g m) -> k g m", g=1),
            BF16,
        )
        whole = slice(0, 1)
        add_up_and_down(unit_images, whole)
        add_centre(unit_images, whole)
        divide_up_down(unit_images, whole)
        repeat_end_columns(unit_images, whole)
        add_left_and_right(unit_images, whole)
        finish_mean(unit_images, whole)
        nc.scalar.activation(out=b_f32[:], in_=b_raw[:], func=COPY)

        turn_x(0)
        regroup(0)
        turn_x(1)
        regroup(1)
        mean_by_matrix(0)
        mean_by_matrix(1)
        bands = []
        for n in range(BATCH):
            top, bottom = matrix_rows[n]
            bands.append(
                mean_by_adds(
                    "band%d" % n,
                    x_pad[:, n : n + 1],
                    top - 1,
                    SIDE - top - bottom,
                    PACK,
                    mean[:, n : n + 1, top : SIDE - bottom, :].rearrange("p n i r -> p n (i r)"),
                    F32,
                )
            )
        add_up_and_down(bands[0], whole)
        quantise_x(0)
        add_up_and_down(bands[1], whole)
        add_centre(bands[0], whole)
        quantise_x(1)
        add_centre(bands[1], whole)
        for step in (
            divide_up_down,
            repeat_end_columns,
            add_left_and_right,
            finish_mean,
        ):
            for band in bands:
                step(band, whole)
        for t in range(PACK):
            turn_weights(t)
        idle_sums = psum.tile([P, PIXELS], F32, name="idle_sums", tag="bank3")
        for i in range(WARM_PASSES):
            nc.tensor.matmul_mx(
                out=idle_sums[:],
                lhsT=x_codes[:, 0, 0:P].bitcast(FP8X4),
                lhsT_scale=x_scales[:, 0, 0:P],
                rhs=x_codes[:, 0, :].bitcast(FP8X4),
                rhs_scale=x_scales[:, 0, :],
                start=True,
                stop=True,
            )
        quantise_mean(0)
        quantise_weights(0)
        quantise_mean(1)
        for t in range(1, PACK):
            quantise_weights(t)
        for t in range(PACK):
            for n in range(BATCH):
                multiply(n, t, 0)
                multiply(n, t, 1)
                relu_with_bias(n, t)
            for n in range(BATCH):
                add_x_and_store(n, t)
